import numpy as np
import ml_dtypes


def mxq(x, axis, fmt="e4m3"):
    dtype, down = {"e4m3": (ml_dtypes.float8_e4m3fn, 7), "e5m2": (ml_dtypes.float8_e5m2, 14)}[fmt]
    v = np.moveaxis(np.asarray(x, np.float32).astype(ml_dtypes.bfloat16).astype(np.float64), axis, -1)
    blocks = v.reshape(v.shape[:-1] + (-1, 32))
    amax = np.abs(blocks).max(-1, keepdims=True)
    byte = np.maximum(np.where(amax > 0, np.frexp(amax)[1] - 1 + 127, 0) - down, 1)
    scale = np.exp2(byte - 127.0)
    codes = (blocks / scale).astype(np.float32).astype(dtype).astype(np.float64)
    return np.moveaxis((codes * scale).reshape(v.shape), -1, axis)


WIDE = False


def mx_kscale(k):
    if not WIDE:
        return np.ones(k)
    levels = np.array([10, -10, 5, -5, 0])
    a = np.random.permutation(np.resize(levels, k // 512 * 4)).reshape(k // 512, 4)
    idx = np.arange(k)
    return np.exp2(a[idx // 512, idx % 128 // 32])


BF16 = ml_dtypes.bfloat16


def bf(x):
    return np.asarray(x, np.float32).astype(BF16)


def f64(x):
    return np.asarray(x).astype(np.float64)


NS, GH, GW, DI, DO, NO = 32, 4, 4, 512, 128, 128
HW = GH * GW
NIN = NS * HW
EPS = 1e-8


def squash(s):
    n2 = np.sum(s * s, axis=-1, keepdims=True)
    return (n2 / (1.0 + n2)) * s / np.sqrt(n2 + EPS)


def softmax(z):
    e = np.exp(z - z.max(axis=-1, keepdims=True))
    return e / e.sum(axis=-1, keepdims=True)


def setup_inputs():
    k = mx_kscale(DI)
    a = NO * np.sqrt(3.0 / (np.e * DO * NIN))
    u = np.random.standard_normal((NS, HW, DI)) * k
    return {"x": bf(u.reshape(1, NS * DI, GH, GW)),
            "W": bf(np.random.standard_normal((NS, DO, DI)) * a / np.sqrt(DI) / k),
            "b": bf(np.random.standard_normal((NIN, NO)))}


def reference(x, W, b):
    u = f64(x).reshape(NS, HW, DI)
    pred = mxq(u, 2, "e4m3") @ mxq(f64(W), 2, "e4m3").transpose(0, 2, 1)
    pred = pred.reshape(NIN, DO)
    c = softmax(f64(b))
    s = mxq(c, 0, "e4m3").T @ mxq(pred, 0, "e4m3")
    return squash(s)

@@ -1,0 +1,218 @@
+from contextlib import ExitStack
+
+import concourse.mybir as mybir
+from concourse.masks import make_identity
+
+F32 = mybir.dt.float32
+BF16 = mybir.dt.bfloat16
+I32 = mybir.dt.int32
+U32 = mybir.dt.uint32
+U8 = mybir.dt.uint8
+FP8X4 = mybir.dt.float8_e4m3fn_x4
+ALU = mybir.AluOpType
+ACT = mybir.ActivationFunctionType
+
+P = 128
+PACK = 4
+
+GROUPS = 32
+POSITIONS = 16
+FEATURES = 512
+D_OUT = 128
+CAPS_IN = GROUPS * POSITIONS
+CAPS_OUT = 128
+EPS = 1e-8
+
+FLOPS = 2 * CAPS_IN * D_OUT * FEATURES + 2 * CAPS_OUT * D_OUT * CAPS_IN
+
+ROWS_PER_PARTITION = 2
+UNIT_ROWS = P * ROWS_PER_PARTITION
+HALVES = 2
+PLANES = ROWS_PER_PARTITION * HALVES
+U_UNITS = CAPS_IN // UNIT_ROWS
+W_UNITS = GROUPS * D_OUT // UNIT_ROWS
+GROUPS_PER_UNIT = UNIT_ROWS // D_OUT
+
+GROUPS_PER_BLOCK = P // POSITIONS
+BLOCKS = GROUPS // GROUPS_PER_BLOCK
+UNITS_PER_BLOCK = GROUPS_PER_BLOCK // GROUPS_PER_UNIT
+DIAG_STEP = P + POSITIONS
+DIAG_WIDTH = GROUPS_PER_BLOCK * DIAG_STEP
+
+FLIP_BANKS = 6
+LEAD = 3
+VECTOR_EVERY = 8
+
+
+def tile_routing_s_kernel(tc, x, W, b, out):
+    nc = tc.nc
+    u_rows = x.rearrange("a (i m) h w -> (a i) (m h w)", i=CAPS_IN)
+    w_rows = W.rearrange("g o f -> (g o) f")
+
+    with ExitStack() as ctx:
+        keep = ctx.enter_context(tc.tile_pool(name="keep", bufs=1))
+        stage = ctx.enter_context(tc.tile_pool(name="stage", bufs=4))
+        flip_psum = ctx.enter_context(tc.psum_pool(name="flip_psum", bufs=FLIP_BANKS))
+        acc_psum = ctx.enter_context(tc.psum_pool(name="acc_psum", bufs=1))
+        ctx.enter_context(tc.manual_schedule())
+
+        b_sb = keep.tile([P, PACK, CAPS_OUT], BF16)
+        nc.sync.dma_start(out=b_sb[:], in_=b.rearrange("(t p) n -> p t n", p=P))
+
+        def load_unit(rows, name):
+            raw = keep.tile([P, ROWS_PER_PARTITION * FEATURES], BF16, name=name)
+            nc.sync.dma_start(
+                out=raw[:], in_=rows.rearrange("(p j) f -> p (j f)", j=ROWS_PER_PARTITION)
+            )
+            return raw
+
+        u_raw = [
+            load_unit(u_rows[v * UNIT_ROWS : (v + 1) * UNIT_ROWS, :], "u_raw%d" % v)
+            for v in range(U_UNITS)
+        ]
+        w_raw = [
+            load_unit(w_rows[v * UNIT_ROWS : (v + 1) * UNIT_ROWS, :], "w_raw%d" % v)
+            for v in range(W_UNITS)
+        ]
+
+        ident = keep.tile([P, P], F32)
+        make_identity(nc, ident[:])
+        eps = keep.tile([P, 1], F32)
+        nc.vector.memset(eps[:], EPS)
+        u_diag = keep.tile([P, BLOCKS, DIAG_WIDTH], U32, align_bytes=64)
+        nc.vector.memset(u_diag[:].bitcast(I32), 0)
+
+        def flip_unit(raw, on_vector):
+            words = raw[:].bitcast(F32)
+            bank = flip_psum.tile([P, PLANES, P], F32, name="bank")
+            for a in range(PLANES):
+                nc.tensor.transpose(bank[:, a, :], words[:, a * P : (a + 1) * P], ident[:])
+            grouped = stage.tile([P, UNIT_ROWS * PACK], BF16, name="grouped", align_bytes=64)
+            dst = grouped[:].bitcast(F32).rearrange("k (r a) -> k r a", a=PLANES)
+            src = bank[:].rearrange("k a r -> k r a")
+            if on_vector:
+                nc.vector.tensor_copy(out=dst, in_=src)
+            else:
+                nc.scalar.copy(out=dst, in_=src)
+            return grouped
+
+        def quantise(grouped, codes, scales):
+            nc.vector.quantize_mx(out=codes.bitcast(FP8X4), scales=scales, in_=grouped)
+
+        neg_max = keep.tile([P, PACK], F32)
+        nc.vector.tensor_reduce(
+            out=neg_max[:], in_=b_sb[:], axis=mybir.AxisListType.X, op=ALU.max, negate=True
+        )
+        expo = keep.tile([P, PACK, CAPS_OUT], F32)
+        sums = keep.tile([P, PACK], F32)
+        for t in range(PACK):
+            nc.scalar.activation(
+                out=expo[:, t, :],
+                in_=b_sb[:, t, :],
+                func=ACT.Exp,
+                bias=neg_max[:, t : t + 1],
+                scale=1.0,
+                accum_out=sums[:, t : t + 1],
+            )
+
+        u_codes = keep.tile([P, CAPS_IN], U32, align_bytes=64)
+        u_scales = keep.tile([P, CAPS_IN], U8, align_bytes=64)
+        u_grouped = [flip_unit(u_raw[v], on_vector=True) for v in range(U_UNITS)]
+        for v in range(U_UNITS):
+            cols = slice(v * UNIT_ROWS, (v + 1) * UNIT_ROWS)
+            quantise(u_grouped[v][:], u_codes[:, cols], u_scales[:, cols])
+        nc.vector.tensor_copy(
+            out=u_diag[:].bitcast(I32).rearrange("k t (r w) -> k t r w", w=DIAG_STEP)[
+                :, :, :, 0:POSITIONS
+            ],
+            in_=u_codes[:].bitcast(I32).rearrange(
+                "k (t r c) -> k t r c", t=BLOCKS, r=GROUPS_PER_BLOCK
+            ),
+        )
+
+        inv_sums = keep.tile([P, PACK], F32)
+        nc.vector.reciprocal(out=inv_sums[:], in_=sums[:])
+        c_grouped = keep.tile([P, CAPS_OUT, PACK], BF16, align_bytes=64)
+        nc.vector.tensor_tensor(
+            out=c_grouped[:],
+            in0=expo[:].rearrange("p t n -> p n t"),
+            in1=inv_sums[:].unsqueeze(1).to_broadcast([P, CAPS_OUT, PACK]),
+            op=ALU.mult,
+        )
+        c_codes = keep.tile([P, CAPS_OUT], U32, align_bytes=64)
+        c_scales = keep.tile([P, CAPS_OUT], U8, align_bytes=64)
+        quantise(c_grouped[:].rearrange("p n t -> p (n t)"), c_codes[:], c_scales[:])
+
+        w_codes = [
+            keep.tile([P, UNIT_ROWS], U32, name="w_codes%d" % v, align_bytes=64)
+            for v in range(W_UNITS)
+        ]
+        w_scales = [
+            keep.tile([P, UNIT_ROWS], U8, name="w_scales%d" % v, align_bytes=64)
+            for v in range(W_UNITS)
+        ]
+        pred_ps = acc_psum.tile([P, BLOCKS, D_OUT], F32)
+
+        def multiply_block(t):
+            for r in range(GROUPS_PER_BLOCK):
+                v, half = divmod(t * GROUPS_PER_BLOCK + r, GROUPS_PER_UNIT)
+                cols = slice(half * D_OUT, (half + 1) * D_OUT)
+                nc.tensor.matmul_mx(
+                    out=pred_ps[:, t, :],
+                    lhsT=u_diag[:, t, r * P : (r + 1) * P].bitcast(FP8X4),
+                    lhsT_scale=u_scales[:, t * P : (t + 1) * P],
+                    rhs=w_codes[v][:, cols].bitcast(FP8X4),
+                    rhs_scale=w_scales[v][:, cols],
+                    start=(r == 0),
+                    stop=(r == GROUPS_PER_BLOCK - 1),
+                )
+
+        w_grouped = [None] * W_UNITS
+        for v in range(W_UNITS):
+            if v > 0:
+                quantise(w_grouped[v - 1][:], w_codes[v - 1][:], w_scales[v - 1][:])
+            w_grouped[v] = flip_unit(w_raw[v], on_vector=(v % VECTOR_EVERY == VECTOR_EVERY // 2))
+            if v % UNITS_PER_BLOCK == LEAD and v > UNITS_PER_BLOCK:
+                multiply_block(v // UNITS_PER_BLOCK - 1)
+        quantise(w_grouped[W_UNITS - 1][:], w_codes[W_UNITS - 1][:], w_scales[W_UNITS - 1][:])
+        table_warm = keep.tile([P, 1], F32)
+        nc.scalar.activation(out=table_warm[:], in_=eps[:], func=ACT.Sqrt)
+        multiply_block(BLOCKS - 1)
+
+        pred_grouped = keep.tile([P, D_OUT, PACK], BF16, align_bytes=64)
+        nc.vector.tensor_copy(out=pred_grouped[:], in_=pred_ps[:].rearrange("p t d -> p d t"))
+        pred_codes = keep.tile([P, D_OUT], U32, align_bytes=64)
+        pred_scales = keep.tile([P, D_OUT], U8, align_bytes=64)
+        quantise(pred_grouped[:].rearrange("p d t -> p (d t)"), pred_codes[:], pred_scales[:])
+        s_ps = acc_psum.tile([P, D_OUT], F32)
+        nc.tensor.matmul_mx(
+            out=s_ps[:],
+            lhsT=c_codes[:].bitcast(FP8X4),
+            lhsT_scale=c_scales[:],
+            rhs=pred_codes[:].bitcast(FP8X4),
+            rhs_scale=pred_scales[:],
+            start=True,
+            stop=True,
+        )
+
+        squares = keep.tile([P, D_OUT], F32)
+        norm2 = keep.tile([P, 1], F32)
+        nc.scalar.activation(out=squares[:], in_=s_ps[:], func=ACT.Square, accum_out=norm2[:])
+        root = keep.tile([P, 1], F32)
+        nc.scalar.activation(out=root[:], in_=norm2[:], func=ACT.Sqrt, bias=eps[:], scale=1.0)
+        denom = keep.tile([P, 1], F32)
+        nc.vector.scalar_tensor_tensor(
+            out=denom[:], in0=norm2[:], scalar=1.0, in1=root[:], op0=ALU.add, op1=ALU.mult
+        )
+        inv_denom = keep.tile([P, 1], F32)
+        nc.vector.reciprocal(out=inv_denom[:], in_=denom[:])
+        out_sb = keep.tile([P, D_OUT], F32)
+        nc.vector.tensor_scalar(
+            out=out_sb[:],
+            in0=s_ps[:],
+            scalar1=norm2[:],
+            scalar2=inv_denom[:],
+            op0=ALU.mult,
+            op1=ALU.mult,
+        )
+        nc.sync.dma_start(out=out, in_=out_sb[:])

@@ -35,12 +35,10 @@ GROUPS_PER_UNIT = UNIT_ROWS // D_OUT
 
 GROUPS_PER_BLOCK = P // POSITIONS
 BLOCKS = GROUPS // GROUPS_PER_BLOCK
-UNITS_PER_BLOCK = GROUPS_PER_BLOCK // GROUPS_PER_UNIT
 DIAG_STEP = P + POSITIONS
 DIAG_WIDTH = GROUPS_PER_BLOCK * DIAG_STEP
 
 FLIP_BANKS = 6
-LEAD = 3
 VECTOR_EVERY = 8
 
 
@@ -172,12 +170,11 @@ def tile_routing_s_kernel(tc, x, W, b, out):
             if v > 0:
                 quantise(w_grouped[v - 1][:], w_codes[v - 1][:], w_scales[v - 1][:])
             w_grouped[v] = flip_unit(w_raw[v], on_vector=(v % VECTOR_EVERY == VECTOR_EVERY // 2))
-            if v % UNITS_PER_BLOCK == LEAD and v > UNITS_PER_BLOCK:
-                multiply_block(v // UNITS_PER_BLOCK - 1)
         quantise(w_grouped[W_UNITS - 1][:], w_codes[W_UNITS - 1][:], w_scales[W_UNITS - 1][:])
         table_warm = keep.tile([P, 1], F32)
         nc.scalar.activation(out=table_warm[:], in_=eps[:], func=ACT.Sqrt)
-        multiply_block(BLOCKS - 1)
+        for t in range(BLOCKS):
+            multiply_block(t)
 
         pred_grouped = keep.tile([P, D_OUT, PACK], BF16, align_bytes=64)
         nc.vector.tensor_copy(out=pred_grouped[:], in_=pred_ps[:].rearrange("p t d -> p d t"))

@@ -25,21 +25,19 @@ EPS = 1e-8
 
 FLOPS = 2 * CAPS_IN * D_OUT * FEATURES + 2 * CAPS_OUT * D_OUT * CAPS_IN
 
-ROWS_PER_PARTITION = 2
-UNIT_ROWS = P * ROWS_PER_PARTITION
+UNIT_ROWS = 2 * P
+SMALL_UNIT_ROWS = P
 HALVES = 2
-PLANES = ROWS_PER_PARTITION * HALVES
-U_UNITS = CAPS_IN // UNIT_ROWS
-W_UNITS = GROUPS * D_OUT // UNIT_ROWS
-GROUPS_PER_UNIT = UNIT_ROWS // D_OUT
 
 GROUPS_PER_BLOCK = P // POSITIONS
 BLOCKS = GROUPS // GROUPS_PER_BLOCK
+BLOCK_ROWS = GROUPS_PER_BLOCK * D_OUT
 DIAG_STEP = P + POSITIONS
 DIAG_WIDTH = GROUPS_PER_BLOCK * DIAG_STEP
 
 FLIP_BANKS = 6
-VECTOR_EVERY = 8
+VECTOR_EVERY = 4
+QUANTISE_LAG = 2
 
 
 def tile_routing_s_kernel(tc, x, W, b, out):
@@ -58,20 +56,22 @@ def tile_routing_s_kernel(tc, x, W, b, out):
         nc.sync.dma_start(out=b_sb[:], in_=b.rearrange("(t p) n -> p t n", p=P))
 
         def load_unit(rows, name):
-            raw = keep.tile([P, ROWS_PER_PARTITION * FEATURES], BF16, name=name)
+            per_partition = rows.shape[0] // P
+            raw = keep.tile([P, per_partition * FEATURES], BF16, name=name)
             nc.sync.dma_start(
-                out=raw[:], in_=rows.rearrange("(p j) f -> p (j f)", j=ROWS_PER_PARTITION)
+                out=raw[:], in_=rows.rearrange("(p j) f -> p (j f)", j=per_partition)
             )
             return raw
 
-        u_raw = [
-            load_unit(u_rows[v * UNIT_ROWS : (v + 1) * UNIT_ROWS, :], "u_raw%d" % v)
-            for v in range(U_UNITS)
-        ]
-        w_raw = [
-            load_unit(w_rows[v * UNIT_ROWS : (v + 1) * UNIT_ROWS, :], "w_raw%d" % v)
-            for v in range(W_UNITS)
-        ]
+        u_raw = []
+        for first in range(0, CAPS_IN, UNIT_ROWS):
+            u_raw.append(load_unit(u_rows[first : first + UNIT_ROWS, :], "u_raw%d" % first))
+        w_unit_rows = [UNIT_ROWS] * (GROUPS * D_OUT // UNIT_ROWS - 1) + [SMALL_UNIT_ROWS] * 2
+        w_raw = []
+        first = 0
+        for n_rows in w_unit_rows:
+            w_raw.append(load_unit(w_rows[first : first + n_rows, :], "w_raw%d" % first))
+            first += n_rows
 
         ident = keep.tile([P, P], F32)
         make_identity(nc, ident[:])
@@ -80,13 +80,14 @@ def tile_routing_s_kernel(tc, x, W, b, out):
         u_diag = keep.tile([P, BLOCKS, DIAG_WIDTH], U32, align_bytes=64)
         nc.vector.memset(u_diag[:].bitcast(I32), 0)
 
-        def flip_unit(raw, on_vector):
+        def flip_unit(raw, n_rows, on_vector):
+            planes = n_rows // P * HALVES
             words = raw[:].bitcast(F32)
-            bank = flip_psum.tile([P, PLANES, P], F32, name="bank")
-            for a in range(PLANES):
+            bank = flip_psum.tile([P, planes, P], F32, name="bank")
+            for a in range(planes):
                 nc.tensor.transpose(bank[:, a, :], words[:, a * P : (a + 1) * P], ident[:])
-            grouped = stage.tile([P, UNIT_ROWS * PACK], BF16, name="grouped", align_bytes=64)
-            dst = grouped[:].bitcast(F32).rearrange("k (r a) -> k r a", a=PLANES)
+            grouped = stage.tile([P, n_rows * PACK], BF16, name="grouped", align_bytes=64)
+            dst = grouped[:].bitcast(F32).rearrange("k (r a) -> k r a", a=planes)
             src = bank[:].rearrange("k a r -> k r a")
             if on_vector:
                 nc.vector.tensor_copy(out=dst, in_=src)
@@ -115,8 +116,8 @@ def tile_routing_s_kernel(tc, x, W, b, out):
 
         u_codes = keep.tile([P, CAPS_IN], U32, align_bytes=64)
         u_scales = keep.tile([P, CAPS_IN], U8, align_bytes=64)
-        u_grouped = [flip_unit(u_raw[v], on_vector=True) for v in range(U_UNITS)]
-        for v in range(U_UNITS):
+        u_grouped = [flip_unit(raw, UNIT_ROWS, on_vector=True) for raw in u_raw]
+        for v in range(len(u_raw)):
             cols = slice(v * UNIT_ROWS, (v + 1) * UNIT_ROWS)
             quantise(u_grouped[v][:], u_codes[:, cols], u_scales[:, cols])
         nc.vector.tensor_copy(
@@ -141,40 +142,53 @@ def tile_routing_s_kernel(tc, x, W, b, out):
         c_scales = keep.tile([P, CAPS_OUT], U8, align_bytes=64)
         quantise(c_grouped[:].rearrange("p n t -> p (n t)"), c_codes[:], c_scales[:])
 
-        w_codes = [
-            keep.tile([P, UNIT_ROWS], U32, name="w_codes%d" % v, align_bytes=64)
-            for v in range(W_UNITS)
-        ]
-        w_scales = [
-            keep.tile([P, UNIT_ROWS], U8, name="w_scales%d" % v, align_bytes=64)
-            for v in range(W_UNITS)
-        ]
+        w_codes = []
+        w_scales = []
+        group_codes = []
+        group_scales = []
+        for v in range(len(w_unit_rows)):
+            codes = keep.tile([P, w_unit_rows[v]], U32, name="w_codes%d" % v, align_bytes=64)
+            scales = keep.tile([P, w_unit_rows[v]], U8, name="w_scales%d" % v, align_bytes=64)
+            w_codes.append(codes)
+            w_scales.append(scales)
+            for first in range(0, w_unit_rows[v], D_OUT):
+                group_codes.append(codes[:, first : first + D_OUT])
+                group_scales.append(scales[:, first : first + D_OUT])
         pred_ps = acc_psum.tile([P, BLOCKS, D_OUT], F32)
 
         def multiply_block(t):
             for r in range(GROUPS_PER_BLOCK):
-                v, half = divmod(t * GROUPS_PER_BLOCK + r, GROUPS_PER_UNIT)
-                cols = slice(half * D_OUT, (half + 1) * D_OUT)
+                g = t * GROUPS_PER_BLOCK + r
                 nc.tensor.matmul_mx(
                     out=pred_ps[:, t, :],
                     lhsT=u_diag[:, t, r * P : (r + 1) * P].bitcast(FP8X4),
                     lhsT_scale=u_scales[:, t * P : (t + 1) * P],
-                    rhs=w_codes[v][:, cols].bitcast(FP8X4),
-                    rhs_scale=w_scales[v][:, cols],
+                    rhs=group_codes[g].bitcast(FP8X4),
+                    rhs_scale=group_scales[g],
                     start=(r == 0),
                     stop=(r == GROUPS_PER_BLOCK - 1),
                 )
 
-        w_grouped = [None] * W_UNITS
-        for v in range(W_UNITS):
-            if v > 0:
-                quantise(w_grouped[v - 1][:], w_codes[v - 1][:], w_scales[v - 1][:])
-            w_grouped[v] = flip_unit(w_raw[v], on_vector=(v % VECTOR_EVERY == VECTOR_EVERY // 2))
-        quantise(w_grouped[W_UNITS - 1][:], w_codes[W_UNITS - 1][:], w_scales[W_UNITS - 1][:])
+        w_grouped = []
+
+        def quantise_w_unit(v):
+            quantise(w_grouped[v][:], w_codes[v][:], w_scales[v][:])
+
+        rows_flipped = 0
+        for v in range(len(w_unit_rows)):
+            if v >= QUANTISE_LAG:
+                quantise_w_unit(v - QUANTISE_LAG)
+            w_grouped.append(
+                flip_unit(w_raw[v], w_unit_rows[v], on_vector=(v % VECTOR_EVERY == 1))
+            )
+            rows_flipped += w_unit_rows[v]
+            if rows_flipped % BLOCK_ROWS == 0 and rows_flipped > BLOCK_ROWS:
+                multiply_block(rows_flipped // BLOCK_ROWS - 2)
+        for v in range(len(w_unit_rows) - QUANTISE_LAG, len(w_unit_rows)):
+            quantise_w_unit(v)
         table_warm = keep.tile([P, 1], F32)
         nc.scalar.activation(out=table_warm[:], in_=eps[:], func=ACT.Sqrt)
-        for t in range(BLOCKS):
-            multiply_block(t)
+        multiply_block(BLOCKS - 1)
 
         pred_grouped = keep.tile([P, D_OUT, PACK], BF16, align_bytes=64)
         nc.vector.tensor_copy(out=pred_grouped[:], in_=pred_ps[:].rearrange("p t d -> p d t"))

@@ -25,19 +25,18 @@ EPS = 1e-8
 
 FLOPS = 2 * CAPS_IN * D_OUT * FEATURES + 2 * CAPS_OUT * D_OUT * CAPS_IN
 
-UNIT_ROWS = 2 * P
-SMALL_UNIT_ROWS = P
 HALVES = 2
+BANK_PLANES = 4
+
+W_UNIT_ROWS = [512] * 6 + [256] * 2 + [128] * 4
 
 GROUPS_PER_BLOCK = P // POSITIONS
 BLOCKS = GROUPS // GROUPS_PER_BLOCK
+
 BLOCK_ROWS = GROUPS_PER_BLOCK * D_OUT
-DIAG_STEP = P + POSITIONS
-DIAG_WIDTH = GROUPS_PER_BLOCK * DIAG_STEP
+MULTIPLY_LAG = 1536
 
 FLIP_BANKS = 6
-VECTOR_EVERY = 4
-QUANTISE_LAG = 2
 
 
 def tile_routing_s_kernel(tc, x, W, b, out):
@@ -63,13 +62,10 @@ def tile_routing_s_kernel(tc, x, W, b, out):
             )
             return raw
 
-        u_raw = []
-        for first in range(0, CAPS_IN, UNIT_ROWS):
-            u_raw.append(load_unit(u_rows[first : first + UNIT_ROWS, :], "u_raw%d" % first))
-        w_unit_rows = [UNIT_ROWS] * (GROUPS * D_OUT // UNIT_ROWS - 1) + [SMALL_UNIT_ROWS] * 2
+        u_raw = load_unit(u_rows, "u_raw")
         w_raw = []
         first = 0
-        for n_rows in w_unit_rows:
+        for n_rows in W_UNIT_ROWS:
             w_raw.append(load_unit(w_rows[first : first + n_rows, :], "w_raw%d" % first))
             first += n_rows
 
@@ -77,22 +73,38 @@ def tile_routing_s_kernel(tc, x, W, b, out):
         make_identity(nc, ident[:])
         eps = keep.tile([P, 1], F32)
         nc.vector.memset(eps[:], EPS)
-        u_diag = keep.tile([P, BLOCKS, DIAG_WIDTH], U32, align_bytes=64)
-        nc.vector.memset(u_diag[:].bitcast(I32), 0)
+        table_exp = keep.tile([P, 1], F32)
+        nc.scalar.activation(out=table_exp[:], in_=eps[:], func=ACT.Exp)
+        u_diag = keep.tile([P, GROUPS * P], U32, align_bytes=64)
+        half = GROUPS * P // 2
+        nc.vector.memset(u_diag[:, 0:half].bitcast(I32), 0)
+        nc.gpsimd.memset(u_diag[:, half : 2 * half].bitcast(I32), 0)
 
-        def flip_unit(raw, n_rows, on_vector):
+        def flip(raw, n_rows):
             planes = n_rows // P * HALVES
             words = raw[:].bitcast(F32)
-            bank = flip_psum.tile([P, planes, P], F32, name="bank")
-            for a in range(planes):
-                nc.tensor.transpose(bank[:, a, :], words[:, a * P : (a + 1) * P], ident[:])
+            banks = []
+            for a0 in range(0, planes, BANK_PLANES):
+                count = min(BANK_PLANES, planes - a0)
+                bank = flip_psum.tile([P, count, P], F32, name="bank")
+                for a in range(count):
+                    nc.tensor.transpose(
+                        bank[:, a, :], words[:, (a0 + a) * P : (a0 + a + 1) * P], ident[:]
+                    )
+                banks.append((bank, a0, count))
+            return banks
+
+        def gather(banks, n_rows, on_vector):
+            planes = n_rows // P * HALVES
             grouped = stage.tile([P, n_rows * PACK], BF16, name="grouped", align_bytes=64)
             dst = grouped[:].bitcast(F32).rearrange("k (r a) -> k r a", a=planes)
-            src = bank[:].rearrange("k a r -> k r a")
-            if on_vector:
-                nc.vector.tensor_copy(out=dst, in_=src)
-            else:
-                nc.scalar.copy(out=dst, in_=src)
+            for i in range(len(banks)):
+                bank, a0, count = banks[i]
+                src = bank[:].rearrange("k a r -> k r a")
+                if on_vector:
+                    nc.vector.tensor_copy(out=dst[:, :, a0 : a0 + count], in_=src)
+                else:
+                    nc.scalar.copy(out=dst[:, :, a0 : a0 + count], in_=src)
             return grouped
 
         def quantise(grouped, codes, scales):
@@ -116,17 +128,11 @@ def tile_routing_s_kernel(tc, x, W, b, out):
 
         u_codes = keep.tile([P, CAPS_IN], U32, align_bytes=64)
         u_scales = keep.tile([P, CAPS_IN], U8, align_bytes=64)
-        u_grouped = [flip_unit(raw, UNIT_ROWS, on_vector=True) for raw in u_raw]
-        for v in range(len(u_raw)):
-            cols = slice(v * UNIT_ROWS, (v + 1) * UNIT_ROWS)
-            quantise(u_grouped[v][:], u_codes[:, cols], u_scales[:, cols])
+        u_grouped = gather(flip(u_raw, CAPS_IN), CAPS_IN, on_vector=True)
+        quantise(u_grouped[:], u_codes[:], u_scales[:])
         nc.vector.tensor_copy(
-            out=u_diag[:].bitcast(I32).rearrange("k t (r w) -> k t r w", w=DIAG_STEP)[
-                :, :, :, 0:POSITIONS
-            ],
-            in_=u_codes[:].bitcast(I32).rearrange(
-                "k (t r c) -> k t r c", t=BLOCKS, r=GROUPS_PER_BLOCK
-            ),
+            out=u_diag[:].bitcast(I32).rearrange("k (g w) -> k g w", w=P)[:, :, 0:POSITIONS],
+            in_=u_codes[:].bitcast(I32).rearrange("k (g c) -> k g c", c=POSITIONS),
         )
 
         inv_sums = keep.tile([P, PACK], F32)
@@ -142,16 +148,17 @@ def tile_routing_s_kernel(tc, x, W, b, out):
         c_scales = keep.tile([P, CAPS_OUT], U8, align_bytes=64)
         quantise(c_grouped[:].rearrange("p n t -> p (n t)"), c_codes[:], c_scales[:])
 
+        n_units = len(W_UNIT_ROWS)
         w_codes = []
         w_scales = []
         group_codes = []
         group_scales = []
-        for v in range(len(w_unit_rows)):
-            codes = keep.tile([P, w_unit_rows[v]], U32, name="w_codes%d" % v, align_bytes=64)
-            scales = keep.tile([P, w_unit_rows[v]], U8, name="w_scales%d" % v, align_bytes=64)
+        for v in range(n_units):
+            codes = keep.tile([P, W_UNIT_ROWS[v]], U32, name="w_codes%d" % v, align_bytes=64)
+            scales = keep.tile([P, W_UNIT_ROWS[v]], U8, name="w_scales%d" % v, align_bytes=64)
             w_codes.append(codes)
             w_scales.append(scales)
-            for first in range(0, w_unit_rows[v], D_OUT):
+            for first in range(0, W_UNIT_ROWS[v], D_OUT):
                 group_codes.append(codes[:, first : first + D_OUT])
                 group_scales.append(scales[:, first : first + D_OUT])
         pred_ps = acc_psum.tile([P, BLOCKS, D_OUT], F32)
@@ -159,9 +166,10 @@ def tile_routing_s_kernel(tc, x, W, b, out):
         def multiply_block(t):
             for r in range(GROUPS_PER_BLOCK):
                 g = t * GROUPS_PER_BLOCK + r
+                start = g * P - r * POSITIONS
                 nc.tensor.matmul_mx(
                     out=pred_ps[:, t, :],
-                    lhsT=u_diag[:, t, r * P : (r + 1) * P].bitcast(FP8X4),
+                    lhsT=u_diag[:, start : start + P].bitcast(FP8X4),
                     lhsT_scale=u_scales[:, t * P : (t + 1) * P],
                     rhs=group_codes[g].bitcast(FP8X4),
                     rhs_scale=group_scales[g],
@@ -175,20 +183,21 @@ def tile_routing_s_kernel(tc, x, W, b, out):
             quantise(w_grouped[v][:], w_codes[v][:], w_scales[v][:])
 
         rows_flipped = 0
-        for v in range(len(w_unit_rows)):
-            if v >= QUANTISE_LAG:
-                quantise_w_unit(v - QUANTISE_LAG)
-            w_grouped.append(
-                flip_unit(w_raw[v], w_unit_rows[v], on_vector=(v % VECTOR_EVERY == 1))
-            )
-            rows_flipped += w_unit_rows[v]
-            if rows_flipped % BLOCK_ROWS == 0 and rows_flipped > BLOCK_ROWS:
-                multiply_block(rows_flipped // BLOCK_ROWS - 2)
-        for v in range(len(w_unit_rows) - QUANTISE_LAG, len(w_unit_rows)):
-            quantise_w_unit(v)
+        multiplied = 0
+        for v in range(n_units):
+            if v >= 1:
+                quantise_w_unit(v - 1)
+            banks = flip(w_raw[v], W_UNIT_ROWS[v])
+            w_grouped.append(gather(banks, W_UNIT_ROWS[v], on_vector=False))
+            rows_flipped += W_UNIT_ROWS[v]
+            while rows_flipped >= (multiplied + 1) * BLOCK_ROWS + MULTIPLY_LAG:
+                multiply_block(multiplied)
+                multiplied += 1
+        quantise_w_unit(n_units - 1)
         table_warm = keep.tile([P, 1], F32)
         nc.scalar.activation(out=table_warm[:], in_=eps[:], func=ACT.Sqrt)
-        multiply_block(BLOCKS - 1)
+        for t in range(multiplied, BLOCKS):
+            multiply_block(t)
 
         pred_grouped = keep.tile([P, D_OUT, PACK], BF16, align_bytes=64)
         nc.vector.tensor_copy(out=pred_grouped[:], in_=pred_ps[:].rearrange("p t d -> p d t"))

@@ -46,13 +46,13 @@ def tile_routing_s_kernel(tc, x, W, b, out):
 
     with ExitStack() as ctx:
         keep = ctx.enter_context(tc.tile_pool(name="keep", bufs=1))
-        stage = ctx.enter_context(tc.tile_pool(name="stage", bufs=4))
+        stage = ctx.enter_context(tc.tile_pool(name="stage", bufs=8))
         flip_psum = ctx.enter_context(tc.psum_pool(name="flip_psum", bufs=FLIP_BANKS))
         acc_psum = ctx.enter_context(tc.psum_pool(name="acc_psum", bufs=1))
         ctx.enter_context(tc.manual_schedule())
 
         b_sb = keep.tile([P, PACK, CAPS_OUT], BF16)
-        nc.sync.dma_start(out=b_sb[:], in_=b.rearrange("(t p) n -> p t n", p=P))
+        nc.scalar.dma_start(out=b_sb[:], in_=b.rearrange("(t p) n -> p t n", p=P))
 
         def load_unit(rows, name):
             per_partition = rows.shape[0] // P
@@ -76,9 +76,7 @@ def tile_routing_s_kernel(tc, x, W, b, out):
         table_exp = keep.tile([P, 1], F32)
         nc.scalar.activation(out=table_exp[:], in_=eps[:], func=ACT.Exp)
         u_diag = keep.tile([P, GROUPS * P], U32, align_bytes=64)
-        half = GROUPS * P // 2
-        nc.vector.memset(u_diag[:, 0:half].bitcast(I32), 0)
-        nc.gpsimd.memset(u_diag[:, half : 2 * half].bitcast(I32), 0)
+        nc.vector.memset(u_diag[:].bitcast(I32), 0)
 
         def flip(raw, n_rows):
             planes = n_rows // P * HALVES
@@ -101,7 +99,7 @@ def tile_routing_s_kernel(tc, x, W, b, out):
             for i in range(len(banks)):
                 bank, a0, count = banks[i]
                 src = bank[:].rearrange("k a r -> k r a")
-                if on_vector:
+                if on_vector[i]:
                     nc.vector.tensor_copy(out=dst[:, :, a0 : a0 + count], in_=src)
                 else:
                     nc.scalar.copy(out=dst[:, :, a0 : a0 + count], in_=src)
@@ -128,7 +126,7 @@ def tile_routing_s_kernel(tc, x, W, b, out):
 
         u_codes = keep.tile([P, CAPS_IN], U32, align_bytes=64)
         u_scales = keep.tile([P, CAPS_IN], U8, align_bytes=64)
-        u_grouped = gather(flip(u_raw, CAPS_IN), CAPS_IN, on_vector=True)
+        u_grouped = gather(flip(u_raw, CAPS_IN), CAPS_IN, on_vector=[True, False])
         quantise(u_grouped[:], u_codes[:], u_scales[:])
         nc.vector.tensor_copy(
             out=u_diag[:].bitcast(I32).rearrange("k (g w) -> k g w", w=P)[:, :, 0:POSITIONS],
@@ -188,14 +186,14 @@ def tile_routing_s_kernel(tc, x, W, b, out):
             if v >= 1:
                 quantise_w_unit(v - 1)
             banks = flip(w_raw[v], W_UNIT_ROWS[v])
-            w_grouped.append(gather(banks, W_UNIT_ROWS[v], on_vector=False))
+            w_grouped.append(gather(banks, W_UNIT_ROWS[v], on_vector=[False, v == 3]))
             rows_flipped += W_UNIT_ROWS[v]
             while rows_flipped >= (multiplied + 1) * BLOCK_ROWS + MULTIPLY_LAG:
                 multiply_block(multiplied)
                 multiplied += 1
         quantise_w_unit(n_units - 1)
         table_warm = keep.tile([P, 1], F32)
-        nc.scalar.activation(out=table_warm[:], in_=eps[:], func=ACT.Sqrt)
+        nc.scalar.activation(out=table_warm[:], in_=eps[:], func=ACT.Abs_reciprocal_sqrt)
         for t in range(multiplied, BLOCKS):
             multiply_block(t)
 
@@ -218,11 +216,15 @@ def tile_routing_s_kernel(tc, x, W, b, out):
         squares = keep.tile([P, D_OUT], F32)
         norm2 = keep.tile([P, 1], F32)
         nc.scalar.activation(out=squares[:], in_=s_ps[:], func=ACT.Square, accum_out=norm2[:])
-        root = keep.tile([P, 1], F32)
-        nc.scalar.activation(out=root[:], in_=norm2[:], func=ACT.Sqrt, bias=eps[:], scale=1.0)
+        inv_root = keep.tile([P, 1], F32)
+        nc.scalar.activation(
+            out=inv_root[:], in_=norm2[:], func=ACT.Abs_reciprocal_sqrt, bias=eps[:], scale=1.0
+        )
+        gain = keep.tile([P, 1], F32)
+        nc.scalar.activation(out=gain[:], in_=inv_root[:], func=ACT.Copy, scale=norm2[:])
         denom = keep.tile([P, 1], F32)
-        nc.vector.scalar_tensor_tensor(
-            out=denom[:], in0=norm2[:], scalar=1.0, in1=root[:], op0=ALU.add, op1=ALU.mult
+        nc.vector.tensor_scalar(
+            out=denom[:], in0=norm2[:], scalar1=1.0, scalar2=None, op0=ALU.add
         )
         inv_denom = keep.tile([P, 1], F32)
         nc.vector.reciprocal(out=inv_denom[:], in_=denom[:])
@@ -230,8 +232,8 @@ def tile_routing_s_kernel(tc, x, W, b, out):
         nc.vector.tensor_scalar(
             out=out_sb[:],
             in0=s_ps[:],
-            scalar1=norm2[:],
-            scalar2=inv_denom[:],
+            scalar1=inv_denom[:],
+            scalar2=gain[:],
             op0=ALU.mult,
             op1=ALU.mult,
         )

@@ -127,20 +127,19 @@ def tile_routing_s_kernel(tc, x, W, b, out):
         u_codes = keep.tile([P, CAPS_IN], U32, align_bytes=64)
         u_scales = keep.tile([P, CAPS_IN], U8, align_bytes=64)
         u_grouped = gather(flip(u_raw, CAPS_IN), CAPS_IN, on_vector=[True, False])
-        quantise(u_grouped[:], u_codes[:], u_scales[:])
-        nc.vector.tensor_copy(
-            out=u_diag[:].bitcast(I32).rearrange("k (g w) -> k g w", w=P)[:, :, 0:POSITIONS],
-            in_=u_codes[:].bitcast(I32).rearrange("k (g c) -> k g c", c=POSITIONS),
-        )
-
         inv_sums = keep.tile([P, PACK], F32)
         nc.vector.reciprocal(out=inv_sums[:], in_=sums[:])
+        quantise(u_grouped[:], u_codes[:], u_scales[:])
         c_grouped = keep.tile([P, CAPS_OUT, PACK], BF16, align_bytes=64)
         nc.vector.tensor_tensor(
             out=c_grouped[:],
             in0=expo[:].rearrange("p t n -> p n t"),
             in1=inv_sums[:].unsqueeze(1).to_broadcast([P, CAPS_OUT, PACK]),
             op=ALU.mult,
+        )
+        nc.vector.tensor_copy(
+            out=u_diag[:].bitcast(I32).rearrange("k (g w) -> k g w", w=P)[:, :, 0:POSITIONS],
+            in_=u_codes[:].bitcast(I32).rearrange("k (g c) -> k g c", c=POSITIONS),
         )
         c_codes = keep.tile([P, CAPS_OUT], U32, align_bytes=64)
         c_scales = keep.tile([P, CAPS_OUT], U8, align_bytes=64)
@@ -183,10 +182,10 @@ def tile_routing_s_kernel(tc, x, W, b, out):
         rows_flipped = 0
         multiplied = 0
         for v in range(n_units):
-            if v >= 1:
-                quantise_w_unit(v - 1)
             banks = flip(w_raw[v], W_UNIT_ROWS[v])
             w_grouped.append(gather(banks, W_UNIT_ROWS[v], on_vector=[False, v == 3]))
+            if v >= 1:
+                quantise_w_unit(v - 1)
             rows_flipped += W_UNIT_ROWS[v]
             while rows_flipped >= (multiplied + 1) * BLOCK_ROWS + MULTIPLY_LAG:
                 multiply_block(multiplied)
@@ -198,10 +197,19 @@ def tile_routing_s_kernel(tc, x, W, b, out):
             multiply_block(t)
 
         pred_grouped = keep.tile([P, D_OUT, PACK], BF16, align_bytes=64)
-        nc.vector.tensor_copy(out=pred_grouped[:], in_=pred_ps[:].rearrange("p t d -> p d t"))
         pred_codes = keep.tile([P, D_OUT], U32, align_bytes=64)
         pred_scales = keep.tile([P, D_OUT], U8, align_bytes=64)
-        quantise(pred_grouped[:].rearrange("p d t -> p (d t)"), pred_codes[:], pred_scales[:])
+        column_halves = [slice(0, D_OUT // 2), slice(D_OUT // 2, D_OUT)]
+        for cols in column_halves:
+            nc.vector.tensor_copy(
+                out=pred_grouped[:, cols, :], in_=pred_ps[:, :, cols].rearrange("p t d -> p d t")
+            )
+        for cols in column_halves:
+            quantise(
+                pred_grouped[:, cols, :].rearrange("p d t -> p (d t)"),
+                pred_codes[:, cols],
+                pred_scales[:, cols],
+            )
         s_ps = acc_psum.tile([P, D_OUT], F32)
         nc.tensor.matmul_mx(
             out=s_ps[:],

@@ -36,6 +36,11 @@ BLOCKS = GROUPS // GROUPS_PER_BLOCK
 BLOCK_ROWS = GROUPS_PER_BLOCK * D_OUT
 MULTIPLY_LAG = 1536
 
+WARM_COLUMNS = 512
+TWO_BF16_ONES = 0x3F803F80
+HEAD_WARM_PASSES = 5
+UNIT_WARM_PASSES = 2
+
 FLIP_BANKS = 6
 
 
@@ -76,6 +81,29 @@ def tile_routing_s_kernel(tc, x, W, b, out):
         table_exp = keep.tile([P, 1], F32)
         nc.scalar.activation(out=table_exp[:], in_=eps[:], func=ACT.Exp)
         u_diag = keep.tile([P, GROUPS * P], U32, align_bytes=64)
+
+        warm_values = keep.tile([P, WARM_COLUMNS * PACK], BF16, align_bytes=64)
+        nc.vector.memset(warm_values[:].bitcast(I32), TWO_BF16_ONES)
+        warm_codes = keep.tile([P, WARM_COLUMNS], U32, align_bytes=64)
+        warm_scales = keep.tile([P, WARM_COLUMNS], U8, align_bytes=64)
+        nc.vector.quantize_mx(
+            out=warm_codes[:].bitcast(FP8X4), scales=warm_scales[:], in_=warm_values[:]
+        )
+        last_ps = acc_psum.tile([P, WARM_COLUMNS], F32)
+
+        def warm(passes):
+            for i in range(passes):
+                nc.tensor.matmul_mx(
+                    out=last_ps[:],
+                    lhsT=warm_codes[:, 0:P].bitcast(FP8X4),
+                    lhsT_scale=warm_scales[:, 0:P],
+                    rhs=warm_codes[:].bitcast(FP8X4),
+                    rhs_scale=warm_scales[:],
+                    start=True,
+                    stop=True,
+                )
+
+        warm(HEAD_WARM_PASSES)
         nc.vector.memset(u_diag[:].bitcast(I32), 0)
 
         def flip(raw, n_rows):
@@ -186,6 +214,8 @@ def tile_routing_s_kernel(tc, x, W, b, out):
             w_grouped.append(gather(banks, W_UNIT_ROWS[v], on_vector=[False, v == 3]))
             if v >= 1:
                 quantise_w_unit(v - 1)
+            if v in (0, 2):
+                warm(UNIT_WARM_PASSES)
             rows_flipped += W_UNIT_ROWS[v]
             while rows_flipped >= (multiplied + 1) * BLOCK_ROWS + MULTIPLY_LAG:
                 multiply_block(multiplied)
@@ -210,9 +240,9 @@ def tile_routing_s_kernel(tc, x, W, b, out):
                 pred_codes[:, cols],
                 pred_scales[:, cols],
             )
-        s_ps = acc_psum.tile([P, D_OUT], F32)
+        s_ps = last_ps[:, 0:D_OUT]
         nc.tensor.matmul_mx(
-            out=s_ps[:],
+            out=s_ps,
             lhsT=c_codes[:].bitcast(FP8X4),
             lhsT_scale=c_scales[:],
             rhs=pred_codes[:].bitcast(FP8X4),
@@ -223,7 +253,7 @@ def tile_routing_s_kernel(tc, x, W, b, out):
 
         squares = keep.tile([P, D_OUT], F32)
         norm2 = keep.tile([P, 1], F32)
-        nc.scalar.activation(out=squares[:], in_=s_ps[:], func=ACT.Square, accum_out=norm2[:])
+        nc.scalar.activation(out=squares[:], in_=s_ps, func=ACT.Square, accum_out=norm2[:])
         inv_root = keep.tile([P, 1], F32)
         nc.scalar.activation(
             out=inv_root[:], in_=norm2[:], func=ACT.Abs_reciprocal_sqrt, bias=eps[:], scale=1.0
@@ -239,7 +269,7 @@ def tile_routing_s_kernel(tc, x, W, b, out):
         out_sb = keep.tile([P, D_OUT], F32)
         nc.vector.tensor_scalar(
             out=out_sb[:],
-            in0=s_ps[:],
+            in0=s_ps,
             scalar1=inv_denom[:],
             scalar2=gain[:],
             op0=ALU.mult,

@@ -36,10 +36,10 @@ BLOCKS = GROUPS // GROUPS_PER_BLOCK
 BLOCK_ROWS = GROUPS_PER_BLOCK * D_OUT
 MULTIPLY_LAG = 1536
 
-WARM_COLUMNS = 512
+WARM_COLUMNS = 256
 TWO_BF16_ONES = 0x3F803F80
-HEAD_WARM_PASSES = 5
-UNIT_WARM_PASSES = 2
+HEAD_WARM_PASSES = 10
+UNIT_WARM_PASSES = 4
 
 FLIP_BANKS = 6
 
@@ -211,7 +211,7 @@ def tile_routing_s_kernel(tc, x, W, b, out):
         multiplied = 0
         for v in range(n_units):
             banks = flip(w_raw[v], W_UNIT_ROWS[v])
-            w_grouped.append(gather(banks, W_UNIT_ROWS[v], on_vector=[False, v == 3]))
+            w_grouped.append(gather(banks, W_UNIT_ROWS[v], on_vector=[False, v in (2, 4)]))
             if v >= 1:
                 quantise_w_unit(v - 1)
             if v in (0, 2):

from contextlib import ExitStack

import concourse.mybir as mybir
from concourse.masks import make_identity

F32 = mybir.dt.float32
BF16 = mybir.dt.bfloat16
I32 = mybir.dt.int32
U32 = mybir.dt.uint32
U8 = mybir.dt.uint8
FP8X4 = mybir.dt.float8_e4m3fn_x4
ALU = mybir.AluOpType
ACT = mybir.ActivationFunctionType

P = 128
PACK = 4

GROUPS = 32
POSITIONS = 16
FEATURES = 512
D_OUT = 128
CAPS_IN = GROUPS * POSITIONS
CAPS_OUT = 128
EPS = 1e-8

FLOPS = 2 * CAPS_IN * D_OUT * FEATURES + 2 * CAPS_OUT * D_OUT * CAPS_IN

HALVES = 2
BANK_PLANES = 4

W_UNIT_ROWS = [512] * 6 + [256] * 2 + [128] * 4

GROUPS_PER_BLOCK = P // POSITIONS
BLOCKS = GROUPS // GROUPS_PER_BLOCK

BLOCK_ROWS = GROUPS_PER_BLOCK * D_OUT
MULTIPLY_LAG = 1536

WARM_COLUMNS = 256
TWO_BF16_ONES = 0x3F803F80
HEAD_WARM_PASSES = 10
UNIT_WARM_PASSES = 4

FLIP_BANKS = 6


def tile_routing_s_kernel(tc, x, W, b, out):
    nc = tc.nc
    u_rows = x.rearrange("a (i m) h w -> (a i) (m h w)", i=CAPS_IN)
    w_rows = W.rearrange("g o f -> (g o) f")

    with ExitStack() as ctx:
        keep = ctx.enter_context(tc.tile_pool(name="keep", bufs=1))
        stage = ctx.enter_context(tc.tile_pool(name="stage", bufs=8))
        flip_psum = ctx.enter_context(tc.psum_pool(name="flip_psum", bufs=FLIP_BANKS))
        acc_psum = ctx.enter_context(tc.psum_pool(name="acc_psum", bufs=1))
        ctx.enter_context(tc.manual_schedule())

        b_sb = keep.tile([P, PACK, CAPS_OUT], BF16)
        nc.scalar.dma_start(out=b_sb[:], in_=b.rearrange("(t p) n -> p t n", p=P))

        def load_unit(rows, name):
            per_partition = rows.shape[0] // P
            raw = keep.tile([P, per_partition * FEATURES], BF16, name=name)
            nc.sync.dma_start(
                out=raw[:], in_=rows.rearrange("(p j) f -> p (j f)", j=per_partition)
            )
            return raw

        u_raw = load_unit(u_rows, "u_raw")
        w_raw = []
        first = 0
        for n_rows in W_UNIT_ROWS:
            w_raw.append(load_unit(w_rows[first : first + n_rows, :], "w_raw%d" % first))
            first += n_rows

        ident = keep.tile([P, P], F32)
        make_identity(nc, ident[:])
        eps = keep.tile([P, 1], F32)
        nc.vector.memset(eps[:], EPS)
        table_exp = keep.tile([P, 1], F32)
        nc.scalar.activation(out=table_exp[:], in_=eps[:], func=ACT.Exp)
        u_diag = keep.tile([P, GROUPS * P], U32, align_bytes=64)

        warm_values = keep.tile([P, WARM_COLUMNS * PACK], BF16, align_bytes=64)
        nc.vector.memset(warm_values[:].bitcast(I32), TWO_BF16_ONES)
        warm_codes = keep.tile([P, WARM_COLUMNS], U32, align_bytes=64)
        warm_scales = keep.tile([P, WARM_COLUMNS], U8, align_bytes=64)
        nc.vector.quantize_mx(
            out=warm_codes[:].bitcast(FP8X4), scales=warm_scales[:], in_=warm_values[:]
        )
        last_ps = acc_psum.tile([P, WARM_COLUMNS], F32)

        def warm(passes):
            for i in range(passes):
                nc.tensor.matmul_mx(
                    out=last_ps[:],
                    lhsT=warm_codes[:, 0:P].bitcast(FP8X4),
                    lhsT_scale=warm_scales[:, 0:P],
                    rhs=warm_codes[:].bitcast(FP8X4),
                    rhs_scale=warm_scales[:],
                    start=True,
                    stop=True,
                )

        warm(HEAD_WARM_PASSES)
        nc.vector.memset(u_diag[:].bitcast(I32), 0)

        def flip(raw, n_rows):
            planes = n_rows // P * HALVES
            words = raw[:].bitcast(F32)
            banks = []
            for a0 in range(0, planes, BANK_PLANES):
                count = min(BANK_PLANES, planes - a0)
                bank = flip_psum.tile([P, count, P], F32, name="bank")
                for a in range(count):
                    nc.tensor.transpose(
                        bank[:, a, :], words[:, (a0 + a) * P : (a0 + a + 1) * P], ident[:]
                    )
                banks.append((bank, a0, count))
            return banks

        def gather(banks, n_rows, on_vector):
            planes = n_rows // P * HALVES
            grouped = stage.tile([P, n_rows * PACK], BF16, name="grouped", align_bytes=64)
            dst = grouped[:].bitcast(F32).rearrange("k (r a) -> k r a", a=planes)
            for i in range(len(banks)):
                bank, a0, count = banks[i]
                src = bank[:].rearrange("k a r -> k r a")
                if on_vector[i]:
                    nc.vector.tensor_copy(out=dst[:, :, a0 : a0 + count], in_=src)
                else:
                    nc.scalar.copy(out=dst[:, :, a0 : a0 + count], in_=src)
            return grouped

        def quantise(grouped, codes, scales):
            nc.vector.quantize_mx(out=codes.bitcast(FP8X4), scales=scales, in_=grouped)

        neg_max = keep.tile([P, PACK], F32)
        nc.vector.tensor_reduce(
            out=neg_max[:], in_=b_sb[:], axis=mybir.AxisListType.X, op=ALU.max, negate=True
        )
        expo = keep.tile([P, PACK, CAPS_OUT], F32)
        sums = keep.tile([P, PACK], F32)
        for t in range(PACK):
            nc.scalar.activation(
                out=expo[:, t, :],
                in_=b_sb[:, t, :],
                func=ACT.Exp,
                bias=neg_max[:, t : t + 1],
                scale=1.0,
                accum_out=sums[:, t : t + 1],
            )

        u_codes = keep.tile([P, CAPS_IN], U32, align_bytes=64)
        u_scales = keep.tile([P, CAPS_IN], U8, align_bytes=64)
        u_grouped = gather(flip(u_raw, CAPS_IN), CAPS_IN, on_vector=[True, False])
        inv_sums = keep.tile([P, PACK], F32)
        nc.vector.reciprocal(out=inv_sums[:], in_=sums[:])
        quantise(u_grouped[:], u_codes[:], u_scales[:])
        c_grouped = keep.tile([P, CAPS_OUT, PACK], BF16, align_bytes=64)
        nc.vector.tensor_tensor(
            out=c_grouped[:],
            in0=expo[:].rearrange("p t n -> p n t"),
            in1=inv_sums[:].unsqueeze(1).to_broadcast([P, CAPS_OUT, PACK]),
            op=ALU.mult,
        )
        nc.vector.tensor_copy(
            out=u_diag[:].bitcast(I32).rearrange("k (g w) -> k g w", w=P)[:, :, 0:POSITIONS],
            in_=u_codes[:].bitcast(I32).rearrange("k (g c) -> k g c", c=POSITIONS),
        )
        c_codes = keep.tile([P, CAPS_OUT], U32, align_bytes=64)
        c_scales = keep.tile([P, CAPS_OUT], U8, align_bytes=64)
        quantise(c_grouped[:].rearrange("p n t -> p (n t)"), c_codes[:], c_scales[:])

        n_units = len(W_UNIT_ROWS)
        w_codes = []
        w_scales = []
        group_codes = []
        group_scales = []
        for v in range(n_units):
            codes = keep.tile([P, W_UNIT_ROWS[v]], U32, name="w_codes%d" % v, align_bytes=64)
            scales = keep.tile([P, W_UNIT_ROWS[v]], U8, name="w_scales%d" % v, align_bytes=64)
            w_codes.append(codes)
            w_scales.append(scales)
            for first in range(0, W_UNIT_ROWS[v], D_OUT):
                group_codes.append(codes[:, first : first + D_OUT])
                group_scales.append(scales[:, first : first + D_OUT])
        pred_ps = acc_psum.tile([P, BLOCKS, D_OUT], F32)

        def multiply_block(t):
            for r in range(GROUPS_PER_BLOCK):
                g = t * GROUPS_PER_BLOCK + r
                start = g * P - r * POSITIONS
                nc.tensor.matmul_mx(
                    out=pred_ps[:, t, :],
                    lhsT=u_diag[:, start : start + P].bitcast(FP8X4),
                    lhsT_scale=u_scales[:, t * P : (t + 1) * P],
                    rhs=group_codes[g].bitcast(FP8X4),
                    rhs_scale=group_scales[g],
                    start=(r == 0),
                    stop=(r == GROUPS_PER_BLOCK - 1),
                )

        w_grouped = []

        def quantise_w_unit(v):
            quantise(w_grouped[v][:], w_codes[v][:], w_scales[v][:])

        rows_flipped = 0
        multiplied = 0
        for v in range(n_units):
            banks = flip(w_raw[v], W_UNIT_ROWS[v])
            w_grouped.append(gather(banks, W_UNIT_ROWS[v], on_vector=[False, v in (2, 4)]))
            if v >= 1:
                quantise_w_unit(v - 1)
            if v in (0, 2):
                warm(UNIT_WARM_PASSES)
            rows_flipped += W_UNIT_ROWS[v]
            while rows_flipped >= (multiplied + 1) * BLOCK_ROWS + MULTIPLY_LAG:
                multiply_block(multiplied)
                multiplied += 1
        quantise_w_unit(n_units - 1)
        table_warm = keep.tile([P, 1], F32)
        nc.scalar.activation(out=table_warm[:], in_=eps[:], func=ACT.Abs_reciprocal_sqrt)
        for t in range(multiplied, BLOCKS):
            multiply_block(t)

        pred_grouped = keep.tile([P, D_OUT, PACK], BF16, align_bytes=64)
        pred_codes = keep.tile([P, D_OUT], U32, align_bytes=64)
        pred_scales = keep.tile([P, D_OUT], U8, align_bytes=64)
        column_halves = [slice(0, D_OUT // 2), slice(D_OUT // 2, D_OUT)]
        for cols in column_halves:
            nc.vector.tensor_copy(
                out=pred_grouped[:, cols, :], in_=pred_ps[:, :, cols].rearrange("p t d -> p d t")
            )
        for cols in column_halves:
            quantise(
                pred_grouped[:, cols, :].rearrange("p d t -> p (d t)"),
                pred_codes[:, cols],
                pred_scales[:, cols],
            )
        s_ps = last_ps[:, 0:D_OUT]
        nc.tensor.matmul_mx(
            out=s_ps,
            lhsT=c_codes[:].bitcast(FP8X4),
            lhsT_scale=c_scales[:],
            rhs=pred_codes[:].bitcast(FP8X4),
            rhs_scale=pred_scales[:],
            start=True,
            stop=True,
        )

        squares = keep.tile([P, D_OUT], F32)
        norm2 = keep.tile([P, 1], F32)
        nc.scalar.activation(out=squares[:], in_=s_ps, func=ACT.Square, accum_out=norm2[:])
        inv_root = keep.tile([P, 1], F32)
        nc.scalar.activation(
            out=inv_root[:], in_=norm2[:], func=ACT.Abs_reciprocal_sqrt, bias=eps[:], scale=1.0
        )
        gain = keep.tile([P, 1], F32)
        nc.scalar.activation(out=gain[:], in_=inv_root[:], func=ACT.Copy, scale=norm2[:])
        denom = keep.tile([P, 1], F32)
        nc.vector.tensor_scalar(
            out=denom[:], in0=norm2[:], scalar1=1.0, scalar2=None, op0=ALU.add
        )
        inv_denom = keep.tile([P, 1], F32)
        nc.vector.reciprocal(out=inv_denom[:], in_=denom[:])
        out_sb = keep.tile([P, D_OUT], F32)
        nc.vector.tensor_scalar(
            out=out_sb[:],
            in0=s_ps,
            scalar1=inv_denom[:],
            scalar2=gain[:],
            op0=ALU.mult,
            op1=ALU.mult,
        )
        nc.sync.dma_start(out=out, in_=out_sb[:])
